import numpy as np
import ml_dtypes


def mxq(x, axis, fmt="e4m3"):
    dtype, down = {"e4m3": (ml_dtypes.float8_e4m3fn, 7), "e5m2": (ml_dtypes.float8_e5m2, 14)}[fmt]
    v = np.moveaxis(np.asarray(x, np.float32).astype(ml_dtypes.bfloat16).astype(np.float64), axis, -1)
    blocks = v.reshape(v.shape[:-1] + (-1, 32))
    amax = np.abs(blocks).max(-1, keepdims=True)
    byte = np.maximum(np.where(amax > 0, np.frexp(amax)[1] - 1 + 127, 0) - down, 1)
    scale = np.exp2(byte - 127.0)
    codes = (blocks / scale).astype(np.float32).astype(dtype).astype(np.float64)
    return np.moveaxis((codes * scale).reshape(v.shape), -1, axis)


WIDE = False


def mx_kscale(k):
    if not WIDE:
        return np.ones(k)
    levels = np.array([10, -10, 5, -5, 0])
    a = np.random.permutation(np.resize(levels, k // 512 * 4)).reshape(k // 512, 4)
    idx = np.arange(k)
    return np.exp2(a[idx // 512, idx % 128 // 32])


BF16 = ml_dtypes.bfloat16


def bf(x):
    return np.asarray(x, np.float32).astype(BF16)


def f64(x):
    return np.asarray(x).astype(np.float64)


B, Q, S, D = 16, 256, 512, 512
K = D + D


def sigmoid(v):
    return 1.0 / (1.0 + np.exp(-v))


def setup_inputs():
    t = mx_kscale(D)
    s = np.concatenate([np.ones(D), t])
    return {"query": bf(np.random.standard_normal((B, Q, D)) * 0.25),
            "weighted_ctx": bf(np.random.standard_normal((B, Q, D)) * 0.12 * t),
            "W_lin": bf(np.random.standard_normal((K, D)) * 5.0 / np.sqrt(K) / s[:, None]),
            "b_lin": bf(np.random.standard_normal(D) * 0.3),
            "W_gate": bf(np.random.standard_normal((K, D)) * 5.0 / np.sqrt(K) / s[:, None]),
            "b_gate": bf(np.random.standard_normal(D) * 0.3)}


def reference(query, weighted_ctx, W_lin, b_lin, W_gate, b_gate):
    q = f64(query)
    cat = mxq(np.concatenate([q, f64(weighted_ctx)], axis=2), 2, "e4m3")
    h = np.tanh((cat @ mxq(f64(W_lin), 0, "e4m3")) + f64(b_lin))
    g = sigmoid((cat @ mxq(f64(W_gate), 0, "e4m3")) + f64(b_gate))
    return q * g + h * (1.0 - g)

@@ -1,0 +1,258 @@
+from contextlib import ExitStack
+
+import concourse.mybir as mybir
+from concourse.masks import make_identity
+
+F32 = mybir.dt.float32
+BF16 = mybir.dt.bfloat16
+U32 = mybir.dt.uint32
+U8 = mybir.dt.uint8
+FP8X4 = mybir.dt.float8_e4m3fn_x4
+ACT = mybir.ActivationFunctionType
+ALU = mybir.AluOpType
+
+P = 128
+PACK = 4
+K_PASS = P * PACK
+TOKENS = 4096
+D = 512
+PASSES = 2
+GROUP = 512
+TILES = GROUP // P
+GROUPS = TOKENS // GROUP
+HALVES = 2
+UNITS = GROUPS * HALVES
+LEAD = 2
+
+FLOPS = 2 * TOKENS * (PASSES * K_PASS) * (2 * D)
+
+
+def tile_smcmr_pb_t_kernel(tc, query, weighted_ctx, W_lin, b_lin, W_gate, b_gate, out):
+    nc = tc.nc
+    with ExitStack() as ctx:
+        ctx.enter_context(tc.manual_schedule())
+        const = ctx.enter_context(tc.tile_pool(name="const", bufs=1))
+        inputs = ctx.enter_context(tc.tile_pool(name="inputs", bufs=1))
+        weights = ctx.enter_context(tc.tile_pool(name="weights", bufs=1))
+        stage = ctx.enter_context(tc.tile_pool(name="stage", bufs=3))
+        acts = ctx.enter_context(tc.tile_pool(name="acts", bufs=2))
+        results = ctx.enter_context(tc.tile_pool(name="results", bufs=2))
+        psum_in = ctx.enter_context(tc.psum_pool(name="psum_in", bufs=2))
+        psum_acc = ctx.enter_context(tc.psum_pool(name="psum_acc", bufs=4))
+        psum_out = ctx.enter_context(tc.psum_pool(name="psum_out", bufs=2))
+
+        by_group = "(G p i) f -> G p (i f)"
+        q_rows = query.flatten_outer_dims().rearrange(by_group, p=P, i=TILES)
+        c_rows = weighted_ctx.flatten_outer_dims().rearrange(by_group, p=P, i=TILES)
+        out_rows = out.flatten_outer_dims().rearrange(by_group, p=P, i=TILES)
+
+        ident = const.tile([P, P], F32)
+        make_identity(nc, ident[:])
+        bias_rows = const.tile([P, 2 * P], BF16)
+        nc.vector.memset(bias_rows[:], 0.0)
+        zero = const.tile([P, 1], F32)
+        nc.vector.memset(zero[:], 0.0)
+        warm = const.tile([P, 1], F32)
+        nc.scalar.activation(out=warm[:], in_=zero[:], func=ACT.Sigmoid)
+        nc.sync.dma_start(out=bias_rows[0:2, :], in_=b_lin.rearrange("(u w) -> u w", u=2))
+        nc.sync.dma_start(out=bias_rows[2:4, :], in_=b_gate.rearrange("(u w) -> u w", u=2))
+
+        q_sb = {}
+        c_sb = {}
+
+        def load_group(G):
+            q_sb[G] = inputs.tile([P, TILES * D], BF16, name="q%d" % G)
+            nc.sync.dma_start(out=q_sb[G][:], in_=q_rows[G])
+            c_sb[G] = inputs.tile([P, TILES * D], BF16, name="c%d" % G)
+            nc.sync.dma_start(out=c_sb[G][:], in_=c_rows[G])
+
+        def load_weight(W, name):
+            raw = weights.tile([P, PASSES * PACK * D], BF16, name=name)
+            nc.sync.dma_start(
+                out=raw[:].rearrange("p (a r) -> p a r", a=PASSES * 2),
+                in_=W.rearrange("(a p e) n -> p a (e n)", p=P, e=2),
+            )
+            return raw
+
+        load_group(0)
+        raw_gate = load_weight(W_gate, "raw_gate")
+        raw_lin = load_weight(W_lin, "raw_lin")
+        for G in range(1, GROUPS):
+            load_group(G)
+
+        bias_bank = psum_in.tile([P, 2, 2 * P], F32, tag="xt")
+        nc.tensor.transpose(out=bias_bank[:, 0, 0:P], in_=bias_rows[:].bitcast(F32), identity=ident[:])
+        bias_pairs = bias_bank[:].rearrange("p u c -> p (u c)").bitcast(BF16)
+        bias_lin = const.tile([P, PACK], F32)
+        nc.vector.tensor_copy(out=bias_lin[:], in_=bias_pairs[:, 0:PACK])
+        bias_gate_neg = const.tile([P, PACK], F32)
+        nc.vector.tensor_scalar_mul(out=bias_gate_neg[:], in0=bias_pairs[:, PACK : 2 * PACK], scalar1=-1.0)
+
+        W_COLS = HALVES * PASSES * 2 * P
+        grouped_w = {}
+        codes_w = {}
+        scales_w = {}
+        for name in ("gate", "lin"):
+            grouped_w[name] = weights.tile([P, W_COLS * PACK], BF16, name="grouped_" + name, align_bytes=64)
+            codes_w[name] = weights.tile([P, W_COLS], U32, name="codes_" + name, align_bytes=64)
+            scales_w[name] = weights.tile([P, W_COLS], U8, name="scales_" + name, align_bytes=64)
+
+        def regroup_weight(copy, raw, name, half):
+            rows = raw[:].rearrange("p (g t n) -> p g t n", g=PASSES, t=PACK)
+            words = grouped_w[name][:].rearrange(
+                "p (u g e j t) -> p u g e j t", u=HALVES, g=PASSES, e=2, t=PACK
+            )
+            for g in range(PASSES):
+                copy(
+                    out=words[:, half, g],
+                    in_=rows[:, g, :, half * 2 * P : (half + 1) * 2 * P].rearrange("p t (j e) -> p e j t", e=2),
+                )
+
+        def quantise_weight(name, half):
+            cols = slice(half * PASSES * 2 * P, (half + 1) * PASSES * 2 * P)
+            nc.vector.quantize_mx(
+                out=codes_w[name][:, cols].bitcast(FP8X4),
+                scales=scales_w[name][:, cols],
+                in_=grouped_w[name][:, half * PASSES * 2 * P * PACK : (half + 1) * PASSES * 2 * P * PACK],
+            )
+
+        grouped = {}
+        codes = {}
+        scales = {}
+        keep = {}
+        cand = {}
+        delta = {}
+        banks_out = {}
+        result = {}
+
+        def transpose_in(v):
+            G, g = divmod(v, PASSES)
+            if g == 0:
+                grouped[G] = stage.tile([P, PASSES * GROUP * PACK], BF16, name="grouped", align_bytes=64)
+            words = (q_sb[G] if g == 0 else c_sb[G])[:].bitcast(F32)
+            pairs = grouped[G][:].bitcast(F32).rearrange("p (g c u) -> p g c u", g=PASSES, u=2)
+            for b in range(2):
+                xt = psum_in.tile([P, 2, 2 * P], F32, tag="xt")
+                for u in range(2):
+                    for ii in range(2):
+                        first = (2 * b + ii) * 2 * P + u * P
+                        nc.tensor.transpose(
+                            out=xt[:, u, ii * P : (ii + 1) * P], in_=words[:, first : first + P], identity=ident[:]
+                        )
+                nc.scalar.copy(
+                    out=pairs[:, g, b * 2 * P : (b + 1) * 2 * P, :], in_=xt[:].rearrange("p u c -> p c u")
+                )
+
+        def quantise_in(v):
+            G, g = divmod(v, PASSES)
+            if g == 0:
+                codes[G] = stage.tile([P, PASSES * GROUP], U32, name="codes", align_bytes=64)
+                scales[G] = stage.tile([P, PASSES * GROUP], U8, name="scales", align_bytes=64)
+            nc.vector.quantize_mx(
+                out=codes[G][:, g * GROUP : (g + 1) * GROUP].bitcast(FP8X4),
+                scales=scales[G][:, g * GROUP : (g + 1) * GROUP],
+                in_=grouped[G][:, g * GROUP * PACK : (g + 1) * GROUP * PACK],
+            )
+
+        def product(name, G, half, e):
+            acc = psum_acc.tile([P, GROUP], F32)
+            for g in range(PASSES):
+                first = ((half * PASSES + g) * 2 + e) * P
+                nc.tensor.matmul_mx(
+                    out=acc[:],
+                    lhsT=codes_w[name][:, first : first + P].bitcast(FP8X4),
+                    lhsT_scale=scales_w[name][:, first : first + P],
+                    rhs=codes[G][:, g * GROUP : (g + 1) * GROUP].bitcast(FP8X4),
+                    rhs_scale=scales[G][:, g * GROUP : (g + 1) * GROUP],
+                    start=(g == 0),
+                    stop=(g == PASSES - 1),
+                )
+            return acc
+
+        def gates(s):
+            G, half = divmod(s, HALVES)
+            keep[s] = acts.tile([P, 2, GROUP], F32, name="keep")
+            cand[s] = acts.tile([P, 2, GROUP], F32, name="cand")
+            for e in range(2):
+                t = 2 * half + e
+                acc = product("gate", G, half, e)
+                nc.scalar.activation(
+                    out=keep[s][:, e, :], in_=acc[:], func=ACT.Sigmoid, bias=bias_gate_neg[:, t : t + 1], scale=-1.0
+                )
+            for e in range(2):
+                t = 2 * half + e
+                acc = product("lin", G, half, e)
+                nc.scalar.activation(
+                    out=cand[s][:, e, :], in_=acc[:], func=ACT.Tanh, bias=bias_lin[:, t : t + 1], scale=1.0
+                )
+
+        def difference(s):
+            G, half = divmod(s, HALVES)
+            q_t = grouped[G][:].rearrange("p (g c t) -> p g c t", g=PASSES, t=PACK)
+            delta[s] = acts.tile([P, 2, GROUP], F32, name="delta")
+            nc.vector.tensor_tensor(
+                out=delta[s][:],
+                in0=q_t[:, 0, :, 2 * half : 2 * half + 2].rearrange("p c e -> p e c"),
+                in1=cand[s][:],
+                op=ALU.subtract,
+            )
+
+        def weigh(s):
+            nc.vector.tensor_tensor(out=delta[s][:], in0=keep[s][:], in1=delta[s][:], op=ALU.mult)
+
+        def transpose_out(s):
+            banks_out[s] = []
+            for b in range(2):
+                ot = psum_out.tile([P, 2, 2, P], F32)
+                for ii in range(2):
+                    for e in range(2):
+                        first = (2 * b + ii) * P
+                        nc.tensor.transpose(
+                            out=ot[:, ii, e, :], in_=delta[s][:, e, first : first + P], identity=ident[:]
+                        )
+                banks_out[s].append(ot)
+
+        def finish(s):
+            G, half = divmod(s, HALVES)
+            if half == 0:
+                result[G] = results.tile([P, TILES * D], F32, name="result")
+            by_pair = "p (i u j e) -> p i u j e"
+            o_view = result[G][:].rearrange(by_pair, i=TILES, u=HALVES, e=2)
+            q_view = q_sb[G][:].rearrange(by_pair, i=TILES, u=HALVES, e=2)
+            for b in range(2):
+                nc.vector.tensor_tensor(
+                    out=o_view[:, 2 * b : 2 * b + 2, half],
+                    in0=q_view[:, 2 * b : 2 * b + 2, half],
+                    in1=banks_out[s][b][:].rearrange("p i e j -> p i j e"),
+                    op=ALU.subtract,
+                )
+            if half == HALVES - 1:
+                nc.sync.dma_start(out=out_rows[G], in_=result[G][:])
+
+        for v in range(LEAD):
+            transpose_in(v)
+            quantise_in(v)
+        regroup_weight(nc.vector.tensor_copy, raw_gate, "gate", 0)
+        quantise_weight("gate", 0)
+        regroup_weight(nc.scalar.copy, raw_gate, "gate", 1)
+        regroup_weight(nc.vector.tensor_copy, raw_lin, "lin", 0)
+        quantise_weight("lin", 0)
+        quantise_weight("gate", 1)
+        regroup_weight(nc.vector.tensor_copy, raw_lin, "lin", 1)
+        quantise_weight("lin", 1)
+
+        for k in range(UNITS + 2):
+            if k + LEAD < UNITS:
+                transpose_in(k + LEAD)
+            if k >= 2:
+                transpose_out(k - 2)
+            if k < UNITS:
+                gates(k)
+            if 1 <= k <= UNITS:
+                difference(k - 1)
+            if k + LEAD < UNITS:
+                quantise_in(k + LEAD)
+            if 1 <= k <= UNITS:
+                weigh(k - 1)
+            if k >= 2:
+                finish(k - 2)

@@ -23,6 +23,7 @@ GROUPS = TOKENS // GROUP
 HALVES = 2
 UNITS = GROUPS * HALVES
 LEAD = 2
+VECTOR_TOKENS = 256
 
 FLOPS = 2 * TOKENS * (PASSES * K_PASS) * (2 * D)
 
@@ -75,8 +76,8 @@ def tile_smcmr_pb_t_kernel(tc, query, weighted_ctx, W_lin, b_lin, W_gate, b_gate
             return raw
 
         load_group(0)
-        raw_gate = load_weight(W_gate, "raw_gate")
         raw_lin = load_weight(W_lin, "raw_lin")
+        raw_gate = load_weight(W_gate, "raw_gate")
         for G in range(1, GROUPS):
             load_group(G)
 
@@ -175,27 +176,28 @@ def tile_smcmr_pb_t_kernel(tc, query, weighted_ctx, W_lin, b_lin, W_gate, b_gate
             cand[s] = acts.tile([P, 2, GROUP], F32, name="cand")
             for e in range(2):
                 t = 2 * half + e
-                acc = product("gate", G, half, e)
-                nc.scalar.activation(
-                    out=keep[s][:, e, :], in_=acc[:], func=ACT.Sigmoid, bias=bias_gate_neg[:, t : t + 1], scale=-1.0
-                )
-            for e in range(2):
-                t = 2 * half + e
                 acc = product("lin", G, half, e)
                 nc.scalar.activation(
                     out=cand[s][:, e, :], in_=acc[:], func=ACT.Tanh, bias=bias_lin[:, t : t + 1], scale=1.0
+                )
+            for e in range(2):
+                t = 2 * half + e
+                acc = product("gate", G, half, e)
+                nc.scalar.activation(
+                    out=keep[s][:, e, :], in_=acc[:], func=ACT.Sigmoid, bias=bias_gate_neg[:, t : t + 1], scale=-1.0
                 )
 
         def difference(s):
             G, half = divmod(s, HALVES)
             q_t = grouped[G][:].rearrange("p (g c t) -> p g c t", g=PASSES, t=PACK)
             delta[s] = acts.tile([P, 2, GROUP], F32, name="delta")
-            nc.vector.tensor_tensor(
-                out=delta[s][:],
-                in0=q_t[:, 0, :, 2 * half : 2 * half + 2].rearrange("p c e -> p e c"),
-                in1=cand[s][:],
-                op=ALU.subtract,
-            )
+            for engine, tokens in ((nc.gpsimd, slice(VECTOR_TOKENS, GROUP)), (nc.vector, slice(0, VECTOR_TOKENS))):
+                engine.tensor_tensor(
+                    out=delta[s][:, :, tokens],
+                    in0=q_t[:, 0, tokens, 2 * half : 2 * half + 2].rearrange("p c e -> p e c"),
+                    in1=cand[s][:, :, tokens],
+                    op=ALU.subtract,
+                )
 
         def weigh(s):
             nc.vector.tensor_tensor(out=delta[s][:], in0=keep[s][:], in1=delta[s][:], op=ALU.mult)
@@ -226,33 +228,35 @@ def tile_smcmr_pb_t_kernel(tc, query, weighted_ctx, W_lin, b_lin, W_gate, b_gate
                     in1=banks_out[s][b][:].rearrange("p i e j -> p i j e"),
                     op=ALU.subtract,
                 )
-            if half == HALVES - 1:
-                nc.sync.dma_start(out=out_rows[G], in_=result[G][:])
+                if half == HALVES - 1:
+                    rows = slice(2 * b * D, (2 * b + 2) * D)
+                    nc.sync.dma_start(out=out_rows[G][:, rows], in_=result[G][:, rows])
 
-        for v in range(LEAD):
-            transpose_in(v)
-            quantise_in(v)
+        transpose_in(0)
+        quantise_in(0)
+        transpose_in(1)
+        regroup_weight(nc.vector.tensor_copy, raw_lin, "lin", 0)
+        quantise_in(1)
+        quantise_weight("lin", 0)
+        regroup_weight(nc.scalar.copy, raw_lin, "lin", 1)
         regroup_weight(nc.vector.tensor_copy, raw_gate, "gate", 0)
         quantise_weight("gate", 0)
-        regroup_weight(nc.scalar.copy, raw_gate, "gate", 1)
-        regroup_weight(nc.vector.tensor_copy, raw_lin, "lin", 0)
-        quantise_weight("lin", 0)
-        quantise_weight("gate", 1)
-        regroup_weight(nc.vector.tensor_copy, raw_lin, "lin", 1)
         quantise_weight("lin", 1)
+        regroup_weight(nc.vector.tensor_copy, raw_gate, "gate", 1)
+        quantise_weight("gate", 1)
 
-        for k in range(UNITS + 2):
+        for k in range(UNITS + 3):
             if k + LEAD < UNITS:
                 transpose_in(k + LEAD)
-            if k >= 2:
-                transpose_out(k - 2)
             if k < UNITS:
                 gates(k)
-            if 1 <= k <= UNITS:
+            if 0 <= k - 2 < UNITS:
+                transpose_out(k - 2)
+            if 0 <= k - 3:
+                finish(k - 3)
+            if 0 <= k - 1 < UNITS:
                 difference(k - 1)
             if k + LEAD < UNITS:
                 quantise_in(k + LEAD)
-            if 1 <= k <= UNITS:
+            if 0 <= k - 1 < UNITS:
                 weigh(k - 1)
-            if k >= 2:
-                finish(k - 2)

@@ -55,8 +55,6 @@ def tile_smcmr_pb_t_kernel(tc, query, weighted_ctx, W_lin, b_lin, W_gate, b_gate
         nc.vector.memset(zero[:], 0.0)
         warm = const.tile([P, 1], F32)
         nc.scalar.activation(out=warm[:], in_=zero[:], func=ACT.Sigmoid)
-        nc.sync.dma_start(out=bias_rows[0:2, :], in_=b_lin.rearrange("(u w) -> u w", u=2))
-        nc.sync.dma_start(out=bias_rows[2:4, :], in_=b_gate.rearrange("(u w) -> u w", u=2))
 
         q_sb = {}
         c_sb = {}
@@ -76,18 +74,22 @@ def tile_smcmr_pb_t_kernel(tc, query, weighted_ctx, W_lin, b_lin, W_gate, b_gate
             return raw
 
         load_group(0)
+        nc.sync.dma_start(out=bias_rows[0:2, :], in_=b_lin.rearrange("(u w) -> u w", u=2))
+        nc.sync.dma_start(out=bias_rows[2:4, :], in_=b_gate.rearrange("(u w) -> u w", u=2))
         raw_lin = load_weight(W_lin, "raw_lin")
         raw_gate = load_weight(W_gate, "raw_gate")
         for G in range(1, GROUPS):
             load_group(G)
 
-        bias_bank = psum_in.tile([P, 2, 2 * P], F32, tag="xt")
-        nc.tensor.transpose(out=bias_bank[:, 0, 0:P], in_=bias_rows[:].bitcast(F32), identity=ident[:])
-        bias_pairs = bias_bank[:].rearrange("p u c -> p (u c)").bitcast(BF16)
         bias_lin = const.tile([P, PACK], F32)
-        nc.vector.tensor_copy(out=bias_lin[:], in_=bias_pairs[:, 0:PACK])
         bias_gate_neg = const.tile([P, PACK], F32)
-        nc.vector.tensor_scalar_mul(out=bias_gate_neg[:], in0=bias_pairs[:, PACK : 2 * PACK], scalar1=-1.0)
+
+        def spread_biases():
+            bias_bank = psum_in.tile([P, 2, 2 * P], F32, tag="xt")
+            nc.tensor.transpose(out=bias_bank[:, 0, 0:P], in_=bias_rows[:].bitcast(F32), identity=ident[:])
+            bias_pairs = bias_bank[:].rearrange("p u c -> p (u c)").bitcast(BF16)
+            nc.vector.tensor_copy(out=bias_lin[:], in_=bias_pairs[:, 0:PACK])
+            nc.vector.tensor_scalar_mul(out=bias_gate_neg[:], in0=bias_pairs[:, PACK : 2 * PACK], scalar1=-1.0)
 
         W_COLS = HALVES * PASSES * 2 * P
         grouped_w = {}
@@ -237,6 +239,7 @@ def tile_smcmr_pb_t_kernel(tc, query, weighted_ctx, W_lin, b_lin, W_gate, b_gate
         transpose_in(1)
         regroup_weight(nc.vector.tensor_copy, raw_lin, "lin", 0)
         quantise_in(1)
+        spread_biases()
         quantise_weight("lin", 0)
         regroup_weight(nc.scalar.copy, raw_lin, "lin", 1)
         regroup_weight(nc.vector.tensor_copy, raw_gate, "gate", 0)

@@ -23,7 +23,7 @@ GROUPS = TOKENS // GROUP
 HALVES = 2
 UNITS = GROUPS * HALVES
 LEAD = 2
-VECTOR_TOKENS = 256
+VECTOR_TOKENS = 320
 
 FLOPS = 2 * TOKENS * (PASSES * K_PASS) * (2 * D)
 

from contextlib import ExitStack

import concourse.mybir as mybir
from concourse.masks import make_identity

F32 = mybir.dt.float32
BF16 = mybir.dt.bfloat16
U32 = mybir.dt.uint32
U8 = mybir.dt.uint8
FP8X4 = mybir.dt.float8_e4m3fn_x4
ACT = mybir.ActivationFunctionType
ALU = mybir.AluOpType

P = 128
PACK = 4
K_PASS = P * PACK
TOKENS = 4096
D = 512
PASSES = 2
GROUP = 512
TILES = GROUP // P
GROUPS = TOKENS // GROUP
HALVES = 2
UNITS = GROUPS * HALVES
LEAD = 2
VECTOR_TOKENS = 320

FLOPS = 2 * TOKENS * (PASSES * K_PASS) * (2 * D)


def tile_smcmr_pb_t_kernel(tc, query, weighted_ctx, W_lin, b_lin, W_gate, b_gate, out):
    nc = tc.nc
    with ExitStack() as ctx:
        ctx.enter_context(tc.manual_schedule())
        const = ctx.enter_context(tc.tile_pool(name="const", bufs=1))
        inputs = ctx.enter_context(tc.tile_pool(name="inputs", bufs=1))
        weights = ctx.enter_context(tc.tile_pool(name="weights", bufs=1))
        stage = ctx.enter_context(tc.tile_pool(name="stage", bufs=3))
        acts = ctx.enter_context(tc.tile_pool(name="acts", bufs=2))
        results = ctx.enter_context(tc.tile_pool(name="results", bufs=2))
        psum_in = ctx.enter_context(tc.psum_pool(name="psum_in", bufs=2))
        psum_acc = ctx.enter_context(tc.psum_pool(name="psum_acc", bufs=4))
        psum_out = ctx.enter_context(tc.psum_pool(name="psum_out", bufs=2))

        by_group = "(G p i) f -> G p (i f)"
        q_rows = query.flatten_outer_dims().rearrange(by_group, p=P, i=TILES)
        c_rows = weighted_ctx.flatten_outer_dims().rearrange(by_group, p=P, i=TILES)
        out_rows = out.flatten_outer_dims().rearrange(by_group, p=P, i=TILES)

        ident = const.tile([P, P], F32)
        make_identity(nc, ident[:])
        bias_rows = const.tile([P, 2 * P], BF16)
        nc.vector.memset(bias_rows[:], 0.0)
        zero = const.tile([P, 1], F32)
        nc.vector.memset(zero[:], 0.0)
        warm = const.tile([P, 1], F32)
        nc.scalar.activation(out=warm[:], in_=zero[:], func=ACT.Sigmoid)

        q_sb = {}
        c_sb = {}

        def load_group(G):
            q_sb[G] = inputs.tile([P, TILES * D], BF16, name="q%d" % G)
            nc.sync.dma_start(out=q_sb[G][:], in_=q_rows[G])
            c_sb[G] = inputs.tile([P, TILES * D], BF16, name="c%d" % G)
            nc.sync.dma_start(out=c_sb[G][:], in_=c_rows[G])

        def load_weight(W, name):
            raw = weights.tile([P, PASSES * PACK * D], BF16, name=name)
            nc.sync.dma_start(
                out=raw[:].rearrange("p (a r) -> p a r", a=PASSES * 2),
                in_=W.rearrange("(a p e) n -> p a (e n)", p=P, e=2),
            )
            return raw

        load_group(0)
        nc.sync.dma_start(out=bias_rows[0:2, :], in_=b_lin.rearrange("(u w) -> u w", u=2))
        nc.sync.dma_start(out=bias_rows[2:4, :], in_=b_gate.rearrange("(u w) -> u w", u=2))
        raw_lin = load_weight(W_lin, "raw_lin")
        raw_gate = load_weight(W_gate, "raw_gate")
        for G in range(1, GROUPS):
            load_group(G)

        bias_lin = const.tile([P, PACK], F32)
        bias_gate_neg = const.tile([P, PACK], F32)

        def spread_biases():
            bias_bank = psum_in.tile([P, 2, 2 * P], F32, tag="xt")
            nc.tensor.transpose(out=bias_bank[:, 0, 0:P], in_=bias_rows[:].bitcast(F32), identity=ident[:])
            bias_pairs = bias_bank[:].rearrange("p u c -> p (u c)").bitcast(BF16)
            nc.vector.tensor_copy(out=bias_lin[:], in_=bias_pairs[:, 0:PACK])
            nc.vector.tensor_scalar_mul(out=bias_gate_neg[:], in0=bias_pairs[:, PACK : 2 * PACK], scalar1=-1.0)

        W_COLS = HALVES * PASSES * 2 * P
        grouped_w = {}
        codes_w = {}
        scales_w = {}
        for name in ("gate", "lin"):
            grouped_w[name] = weights.tile([P, W_COLS * PACK], BF16, name="grouped_" + name, align_bytes=64)
            codes_w[name] = weights.tile([P, W_COLS], U32, name="codes_" + name, align_bytes=64)
            scales_w[name] = weights.tile([P, W_COLS], U8, name="scales_" + name, align_bytes=64)

        def regroup_weight(copy, raw, name, half):
            rows = raw[:].rearrange("p (g t n) -> p g t n", g=PASSES, t=PACK)
            words = grouped_w[name][:].rearrange(
                "p (u g e j t) -> p u g e j t", u=HALVES, g=PASSES, e=2, t=PACK
            )
            for g in range(PASSES):
                copy(
                    out=words[:, half, g],
                    in_=rows[:, g, :, half * 2 * P : (half + 1) * 2 * P].rearrange("p t (j e) -> p e j t", e=2),
                )

        def quantise_weight(name, half):
            cols = slice(half * PASSES * 2 * P, (half + 1) * PASSES * 2 * P)
            nc.vector.quantize_mx(
                out=codes_w[name][:, cols].bitcast(FP8X4),
                scales=scales_w[name][:, cols],
                in_=grouped_w[name][:, half * PASSES * 2 * P * PACK : (half + 1) * PASSES * 2 * P * PACK],
            )

        grouped = {}
        codes = {}
        scales = {}
        keep = {}
        cand = {}
        delta = {}
        banks_out = {}
        result = {}

        def transpose_in(v):
            G, g = divmod(v, PASSES)
            if g == 0:
                grouped[G] = stage.tile([P, PASSES * GROUP * PACK], BF16, name="grouped", align_bytes=64)
            words = (q_sb[G] if g == 0 else c_sb[G])[:].bitcast(F32)
            pairs = grouped[G][:].bitcast(F32).rearrange("p (g c u) -> p g c u", g=PASSES, u=2)
            for b in range(2):
                xt = psum_in.tile([P, 2, 2 * P], F32, tag="xt")
                for u in range(2):
                    for ii in range(2):
                        first = (2 * b + ii) * 2 * P + u * P
                        nc.tensor.transpose(
                            out=xt[:, u, ii * P : (ii + 1) * P], in_=words[:, first : first + P], identity=ident[:]
                        )
                nc.scalar.copy(
                    out=pairs[:, g, b * 2 * P : (b + 1) * 2 * P, :], in_=xt[:].rearrange("p u c -> p c u")
                )

        def quantise_in(v):
            G, g = divmod(v, PASSES)
            if g == 0:
                codes[G] = stage.tile([P, PASSES * GROUP], U32, name="codes", align_bytes=64)
                scales[G] = stage.tile([P, PASSES * GROUP], U8, name="scales", align_bytes=64)
            nc.vector.quantize_mx(
                out=codes[G][:, g * GROUP : (g + 1) * GROUP].bitcast(FP8X4),
                scales=scales[G][:, g * GROUP : (g + 1) * GROUP],
                in_=grouped[G][:, g * GROUP * PACK : (g + 1) * GROUP * PACK],
            )

        def product(name, G, half, e):
            acc = psum_acc.tile([P, GROUP], F32)
            for g in range(PASSES):
                first = ((half * PASSES + g) * 2 + e) * P
                nc.tensor.matmul_mx(
                    out=acc[:],
                    lhsT=codes_w[name][:, first : first + P].bitcast(FP8X4),
                    lhsT_scale=scales_w[name][:, first : first + P],
                    rhs=codes[G][:, g * GROUP : (g + 1) * GROUP].bitcast(FP8X4),
                    rhs_scale=scales[G][:, g * GROUP : (g + 1) * GROUP],
                    start=(g == 0),
                    stop=(g == PASSES - 1),
                )
            return acc

        def gates(s):
            G, half = divmod(s, HALVES)
            keep[s] = acts.tile([P, 2, GROUP], F32, name="keep")
            cand[s] = acts.tile([P, 2, GROUP], F32, name="cand")
            for e in range(2):
                t = 2 * half + e
                acc = product("lin", G, half, e)
                nc.scalar.activation(
                    out=cand[s][:, e, :], in_=acc[:], func=ACT.Tanh, bias=bias_lin[:, t : t + 1], scale=1.0
                )
            for e in range(2):
                t = 2 * half + e
                acc = product("gate", G, half, e)
                nc.scalar.activation(
                    out=keep[s][:, e, :], in_=acc[:], func=ACT.Sigmoid, bias=bias_gate_neg[:, t : t + 1], scale=-1.0
                )

        def difference(s):
            G, half = divmod(s, HALVES)
            q_t = grouped[G][:].rearrange("p (g c t) -> p g c t", g=PASSES, t=PACK)
            delta[s] = acts.tile([P, 2, GROUP], F32, name="delta")
            for engine, tokens in ((nc.gpsimd, slice(VECTOR_TOKENS, GROUP)), (nc.vector, slice(0, VECTOR_TOKENS))):
                engine.tensor_tensor(
                    out=delta[s][:, :, tokens],
                    in0=q_t[:, 0, tokens, 2 * half : 2 * half + 2].rearrange("p c e -> p e c"),
                    in1=cand[s][:, :, tokens],
                    op=ALU.subtract,
                )

        def weigh(s):
            nc.vector.tensor_tensor(out=delta[s][:], in0=keep[s][:], in1=delta[s][:], op=ALU.mult)

        def transpose_out(s):
            banks_out[s] = []
            for b in range(2):
                ot = psum_out.tile([P, 2, 2, P], F32)
                for ii in range(2):
                    for e in range(2):
                        first = (2 * b + ii) * P
                        nc.tensor.transpose(
                            out=ot[:, ii, e, :], in_=delta[s][:, e, first : first + P], identity=ident[:]
                        )
                banks_out[s].append(ot)

        def finish(s):
            G, half = divmod(s, HALVES)
            if half == 0:
                result[G] = results.tile([P, TILES * D], F32, name="result")
            by_pair = "p (i u j e) -> p i u j e"
            o_view = result[G][:].rearrange(by_pair, i=TILES, u=HALVES, e=2)
            q_view = q_sb[G][:].rearrange(by_pair, i=TILES, u=HALVES, e=2)
            for b in range(2):
                nc.vector.tensor_tensor(
                    out=o_view[:, 2 * b : 2 * b + 2, half],
                    in0=q_view[:, 2 * b : 2 * b + 2, half],
                    in1=banks_out[s][b][:].rearrange("p i e j -> p i j e"),
                    op=ALU.subtract,
                )
                if half == HALVES - 1:
                    rows = slice(2 * b * D, (2 * b + 2) * D)
                    nc.sync.dma_start(out=out_rows[G][:, rows], in_=result[G][:, rows])

        transpose_in(0)
        quantise_in(0)
        transpose_in(1)
        regroup_weight(nc.vector.tensor_copy, raw_lin, "lin", 0)
        quantise_in(1)
        spread_biases()
        quantise_weight("lin", 0)
        regroup_weight(nc.scalar.copy, raw_lin, "lin", 1)
        regroup_weight(nc.vector.tensor_copy, raw_gate, "gate", 0)
        quantise_weight("gate", 0)
        quantise_weight("lin", 1)
        regroup_weight(nc.vector.tensor_copy, raw_gate, "gate", 1)
        quantise_weight("gate", 1)

        for k in range(UNITS + 3):
            if k + LEAD < UNITS:
                transpose_in(k + LEAD)
            if k < UNITS:
                gates(k)
            if 0 <= k - 2 < UNITS:
                transpose_out(k - 2)
            if 0 <= k - 3:
                finish(k - 3)
            if 0 <= k - 1 < UNITS:
                difference(k - 1)
            if k + LEAD < UNITS:
                quantise_in(k + LEAD)
            if 0 <= k - 1 < UNITS:
                weigh(k - 1)
